import numpy as np
import ml_dtypes


def mxq(x, axis, fmt="e4m3"):
    dtype, down = {"e4m3": (ml_dtypes.float8_e4m3fn, 7), "e5m2": (ml_dtypes.float8_e5m2, 14)}[fmt]
    v = np.moveaxis(np.asarray(x, np.float32).astype(ml_dtypes.bfloat16).astype(np.float64), axis, -1)
    blocks = v.reshape(v.shape[:-1] + (-1, 32))
    amax = np.abs(blocks).max(-1, keepdims=True)
    byte = np.maximum(np.where(amax > 0, np.frexp(amax)[1] - 1 + 127, 0) - down, 1)
    scale = np.exp2(byte - 127.0)
    codes = (blocks / scale).astype(np.float32).astype(dtype).astype(np.float64)
    return np.moveaxis((codes * scale).reshape(v.shape), -1, axis)


WIDE = False


def mx_kscale(k):
    if not WIDE:
        return np.ones(k)
    levels = np.array([10, -10, 5, -5, 0])
    a = np.random.permutation(np.resize(levels, k // 512 * 4)).reshape(k // 512, 4)
    idx = np.arange(k)
    return np.exp2(a[idx // 512, idx % 128 // 32])


BF16 = ml_dtypes.bfloat16


def bf(x):
    return np.asarray(x, np.float32).astype(BF16)


def f64(x):
    return np.asarray(x).astype(np.float64)


B, S, HID, H, HKV, DH = 2, 128, 2048, 16, 16, 128
NH = H + 2 * HKV


def rotate_half(x):
    x1 = x[..., ::2]
    x2 = x[..., 1::2]
    return np.stack((-x2, x1), axis=-1).reshape(x.shape)


def setup_inputs():
    s = mx_kscale(HID)
    inv_freq = 1.0 / (10000.0 ** (np.arange(0, DH, 2) / DH))
    emb = np.repeat(np.outer(np.arange(S), inv_freq), 2, axis=-1)
    return {"hidden_states": bf(np.random.standard_normal((B, S, HID)) * s),
            "cos": bf(np.cos(emb)),
            "sin": bf(np.sin(emb)),
            "w_qkv": bf(np.random.standard_normal((NH * DH, HID)) / np.sqrt(HID) / s[None, :])}


def reference(hidden_states, cos, sin, w_qkv):
    qkv = mxq(f64(hidden_states), 2, "e4m3") @ mxq(f64(w_qkv), 1, "e4m3").T
    qkv = qkv.reshape(B, S, NH, DH)
    q = qkv[:, :, :H]
    k = qkv[:, :, H:H + HKV]
    v = qkv[:, :, H + HKV:]
    cos_s = f64(cos)[:S][None, :, None, :]
    sin_s = f64(sin)[:S][None, :, None, :]
    q = q * cos_s + rotate_half(q) * sin_s
    k = k * cos_s + rotate_half(k) * sin_s
    return q, k, v

@@ -1,0 +1,219 @@
+from contextlib import ExitStack
+
+import concourse.mybir as mybir
+from concourse.masks import make_identity
+
+F32 = mybir.dt.float32
+BF16 = mybir.dt.bfloat16
+U32 = mybir.dt.uint32
+U8 = mybir.dt.uint8
+FP8X4 = mybir.dt.float8_e4m3fn_x4
+MULT = mybir.AluOpType.mult
+ADD = mybir.AluOpType.add
+
+FLOPS = 2 * 256 * 6144 * 2048
+
+P = 128
+NCHUNK = 12
+W_BUFS = 6
+GRP_BUFS = 4
+CODE_BUFS = 4
+OST_BUFS = 10
+T_BANKS = 5
+A_BANKS = 3
+STORE_Q = "sync"
+PIN = True
+
+
+def tile_attention_pa_kernel(tc, hidden_states, cos, sin, w_qkv, out_0, out_1, out_2):
+    nc = tc.nc
+    outs = (out_0, out_1, out_2)
+    order = [(kind, hc) for hc in range(4) for kind in range(3)]
+    with ExitStack() as ctx:
+        const = ctx.enter_context(tc.tile_pool(name="const", bufs=1))
+        wpool = ctx.enter_context(tc.tile_pool(name="wpool", bufs=W_BUFS))
+        gpool = ctx.enter_context(tc.tile_pool(name="gpool", bufs=GRP_BUFS))
+        cpool = ctx.enter_context(tc.tile_pool(name="cpool", bufs=CODE_BUFS))
+        rpool = ctx.enter_context(tc.tile_pool(name="rpool", bufs=2))
+        opool = ctx.enter_context(tc.tile_pool(name="opool", bufs=OST_BUFS))
+        psum_t = ctx.enter_context(tc.psum_pool(name="psum_t", bufs=T_BANKS))
+        psum_a = ctx.enter_context(tc.psum_pool(name="psum_a", bufs=A_BANKS))
+        if PIN:
+            ctx.enter_context(tc.manual_schedule())
+
+        store_eng = {"sync": nc.sync, "gpsimd": nc.gpsimd, "scalar": nc.scalar}[STORE_Q]
+
+        ident = const.tile([P, P], F32)
+        make_identity(nc, ident[:])
+        cos_raw = const.tile([P, P], BF16)
+        sin_raw = const.tile([P, P], BF16)
+        nc.scalar.dma_start(out=cos_raw[:], in_=cos)
+        nc.scalar.dma_start(out=sin_raw[:], in_=sin)
+
+        xraw = const.tile([P, 4096], BF16)
+        x_dram = hidden_states.rearrange("b s k -> s b k")
+        x_sb = xraw[:].rearrange("p (b k) -> p b k", b=2)
+        for hf in range(2):
+            nc.sync.dma_start(out=x_sb[:, :, 1024 * hf:1024 * hf + 1024],
+                              in_=x_dram[:, :, 1024 * hf:1024 * hf + 1024])
+
+        wraws = []
+        for c in range(NCHUNK):
+            kind, hc = order[c]
+            r0 = 2048 * kind + 512 * hc
+            wraw = wpool.tile([P, 8192], BF16)
+            wraws.append(wraw)
+            pieces = 4 if c == 0 else (2 if c == 1 else 1)
+            if pieces == 1:
+                nc.sync.dma_start(out=wraw[:], in_=w_qkv[r0:r0 + 512, :].rearrange("(p j) k -> p (j k)", j=4))
+            else:
+                wid = 2048 // pieces
+                w_sb = wraw[:].rearrange("p (j k) -> p j k", j=4)
+                for i in range(pieces):
+                    nc.sync.dma_start(
+                        out=w_sb[:, :, wid * i:wid * i + wid],
+                        in_=w_qkv[r0:r0 + 512, wid * i:wid * i + wid].rearrange("(p j) k -> p j k", j=4))
+
+        xf = xraw[:].bitcast(F32)
+        xgrp = const.tile([P, 4096], BF16, align_bytes=64)
+        xgf = xgrp[:].bitcast(F32)
+        xc = const.tile([P, 1024], U32, align_bytes=64)
+        xs = const.tile([P, 1024], U8, align_bytes=64)
+        for g in range(4):
+            tpx = psum_t.tile([P, 512], F32, tag="tp")
+            for t in range(4):
+                b, u = t // 2, t % 2
+                nc.tensor.transpose(tpx[:, 128 * t:128 * t + 128],
+                                    xf[:, 1024 * b + 256 * g + 128 * u:1024 * b + 256 * g + 128 * u + 128],
+                                    ident[:])
+            dst = xgf[:, 512 * g:512 * g + 512].rearrange("q (b s u) -> q b s u", b=2, u=2)
+            src = tpx[:].rearrange("q (b u s) -> q b s u", b=2, u=2)
+            if g % 2 == 0:
+                nc.scalar.copy(out=dst, in_=src)
+            else:
+                nc.vector.tensor_copy(out=dst, in_=src)
+        for hf in range(2):
+            nc.vector.quantize_mx(out=xc[:, 512 * hf:512 * hf + 512].bitcast(FP8X4),
+                                  scales=xs[:, 512 * hf:512 * hf + 512],
+                                  in_=xgrp[:, 2048 * hf:2048 * hf + 2048])
+
+        cosd = const.tile([P, P], F32)
+        sind = const.tile([P, P], F32)
+        nc.vector.tensor_copy(out=cosd[:].rearrange("p (e i) -> p e i", e=2),
+                              in_=cos_raw[:].rearrange("p (i e) -> p e i", e=2))
+        sin_v = sin_raw[:].rearrange("p (i e) -> p e i", e=2)
+        nc.vector.tensor_scalar_mul(out=sind[:, 0:64], in0=sin_v[:, 0, :], scalar1=-1.0)
+        nc.vector.tensor_copy(out=sind[:, 64:128], in_=sin_v[:, 1, :])
+
+        grps = {}
+        codes = {}
+        accs = {}
+
+        def transposes(c):
+            wf = wraws[c][:].bitcast(F32)
+            for half in range(2):
+                grp = gpool.tile([P, 4096], BF16, align_bytes=64, tag="grp")
+                grps[(c, half)] = grp
+                gf = grp[:].bitcast(F32)
+                for gg in range(2):
+                    g = 2 * half + gg
+                    for e in range(2):
+                        tp = psum_t.tile([P, 512], F32, tag="tp")
+                        for t in range(4):
+                            j = 2 * (t // 2) + e
+                            u = t % 2
+                            o = 1024 * j + 256 * g + 128 * u
+                            nc.tensor.transpose(tp[:, 128 * t:128 * t + 128], wf[:, o:o + 128], ident[:])
+                        dst = gf[:, 1024 * gg:1024 * gg + 1024].rearrange(
+                            "q (h e r) -> q h e r", h=4, e=2)[:, :, e, :].rearrange("q h (pp t) -> q h pp t", t=4)
+                        src = tp[:].rearrange("q (t h pp) -> q h pp t", t=4, h=4)
+                        nc.scalar.copy(out=dst, in_=src)
+
+        def quantise(c, half):
+            wc = cpool.tile([P, 1024], U32, align_bytes=64, tag="wc")
+            ws = cpool.tile([P, 1024], U8, align_bytes=64, tag="ws")
+            codes[(c, half)] = (wc, ws)
+            nc.vector.quantize_mx(out=wc[:].bitcast(FP8X4), scales=ws[:], in_=grps[(c, half)][:])
+
+        def mx_pass(c, g, b):
+            wc, ws = codes[(c, g // 2)]
+            lo = 512 * (g % 2)
+            xo = 256 * g + 128 * b
+            nc.tensor.matmul_mx(out=accs[(c, b)][:],
+                                lhsT=xc[:, xo:xo + 128].bitcast(FP8X4), lhsT_scale=xs[:, xo:xo + 128],
+                                rhs=wc[:, lo:lo + 512].bitcast(FP8X4), rhs_scale=ws[:, lo:lo + 512],
+                                start=(g == 0), stop=(g == 3))
+
+        def matmuls(c, g_major):
+            for b in range(2):
+                acc = psum_a.tile([P, 512], F32, tag="acc")
+                accs[(c, b)] = acc
+            if g_major:
+                for g in range(4):
+                    for b in range(2):
+                        mx_pass(c, g, b)
+            else:
+                for b in range(2):
+                    for g in range(4):
+                        mx_pass(c, g, b)
+
+        rope_t = {}
+
+        def rope_mults(c, b):
+            acc = accs[(c, b)]
+            t1 = rpool.tile([P, 512], F32, tag="t1")
+            t2 = rpool.tile([P, 512], F32, tag="t2")
+            rope_t[(c, b)] = (t1, t2)
+            nc.vector.tensor_tensor(out=t1[:].rearrange("p (h m) -> p h m", h=4),
+                                    in0=acc[:].rearrange("p (h m) -> p h m", h=4),
+                                    in1=cosd[:].unsqueeze(1).to_broadcast([P, 4, P]), op=MULT)
+            a4 = acc[:].rearrange("p (h e i) -> p h e i", h=4, e=2)
+            t4 = t2[:].rearrange("p (h e i) -> p h e i", h=4, e=2)
+            for e in range(2):
+                nc.vector.tensor_tensor(out=t4[:, :, e, :], in0=a4[:, :, 1 - e, :],
+                                        in1=sind[:, 64 * e:64 * e + 64].unsqueeze(1).to_broadcast([P, 4, 64]),
+                                        op=MULT)
+
+        def rope_add(c, b, ost):
+            t1, t2 = rope_t[(c, b)]
+            nc.vector.tensor_tensor(out=ost[:, 512 * b:512 * b + 512].rearrange("p (h i e) -> p h i e", h=4, e=2),
+                                    in0=t1[:].rearrange("p (h e i) -> p h i e", h=4, e=2),
+                                    in1=t2[:].rearrange("p (h e i) -> p h i e", h=4, e=2), op=ADD)
+
+        def plain_out(c, b, ost, eng):
+            dst = ost[:, 512 * b:512 * b + 512].rearrange("p (h i e) -> p h i e", h=4, e=2)
+            src = accs[(c, b)][:].rearrange("p (h e i) -> p h i e", h=4, e=2)
+            if eng == "s":
+                nc.scalar.copy(out=dst, in_=src)
+            else:
+                nc.vector.tensor_copy(out=dst, in_=src)
+
+        def store(c, ost):
+            kind, hc = order[c]
+            store_eng.dma_start(
+                out=outs[kind].rearrange("b s h l -> s b (h l)")[:, :, 512 * hc:512 * hc + 512],
+                in_=ost[:].rearrange("p (b m) -> p b m", b=2))
+
+        for c in range(NCHUNK + 1):
+            d = c - 1
+            if c < NCHUNK:
+                transposes(c)
+            if d >= 0:
+                matmuls(d, g_major=(d == NCHUNK - 1))
+                ost = opool.tile([P, 1024], F32, tag="ost")
+            roped = d >= 0 and order[d][0] < 2
+            if c < NCHUNK:
+                quantise(c, 0)
+            if roped:
+                rope_mults(d, 0)
+            if c < NCHUNK:
+                quantise(c, 1)
+            if roped:
+                rope_mults(d, 1)
+                rope_add(d, 0, ost)
+                rope_add(d, 1, ost)
+            elif d >= 0:
+                plain_out(d, 0, ost, "s")
+                plain_out(d, 1, ost, "v")
+            if d >= 0:
+                store(d, ost)

@@ -21,8 +21,14 @@ CODE_BUFS = 4
 OST_BUFS = 10
 T_BANKS = 5
 A_BANKS = 3
+R_BUFS = 2
 STORE_Q = "sync"
 PIN = True
+LAYOUT = "nat"
+HALF = False
+VCOPY = ()
+LAST_S = False
+GADD = False
 
 
 def tile_attention_pa_kernel(tc, hidden_states, cos, sin, w_qkv, out_0, out_1, out_2):
@@ -34,7 +40,7 @@ def tile_attention_pa_kernel(tc, hidden_states, cos, sin, w_qkv, out_0, out_1, o
         wpool = ctx.enter_context(tc.tile_pool(name="wpool", bufs=W_BUFS))
         gpool = ctx.enter_context(tc.tile_pool(name="gpool", bufs=GRP_BUFS))
         cpool = ctx.enter_context(tc.tile_pool(name="cpool", bufs=CODE_BUFS))
-        rpool = ctx.enter_context(tc.tile_pool(name="rpool", bufs=2))
+        rpool = ctx.enter_context(tc.tile_pool(name="rpool", bufs=R_BUFS))
         opool = ctx.enter_context(tc.tile_pool(name="opool", bufs=OST_BUFS))
         psum_t = ctx.enter_context(tc.psum_pool(name="psum_t", bufs=T_BANKS))
         psum_a = ctx.enter_context(tc.psum_pool(name="psum_a", bufs=A_BANKS))
@@ -64,15 +70,19 @@ def tile_attention_pa_kernel(tc, hidden_states, cos, sin, w_qkv, out_0, out_1, o
             wraw = wpool.tile([P, 8192], BF16)
             wraws.append(wraw)
             pieces = 4 if c == 0 else (2 if c == 1 else 1)
-            if pieces == 1:
-                nc.sync.dma_start(out=wraw[:], in_=w_qkv[r0:r0 + 512, :].rearrange("(p j) k -> p (j k)", j=4))
-            else:
-                wid = 2048 // pieces
-                w_sb = wraw[:].rearrange("p (j k) -> p j k", j=4)
-                for i in range(pieces):
-                    nc.sync.dma_start(
-                        out=w_sb[:, :, wid * i:wid * i + wid],
-                        in_=w_qkv[r0:r0 + 512, wid * i:wid * i + wid].rearrange("(p j) k -> p j k", j=4))
+            wid = 2048 // pieces
+            w_sb = wraw[:].rearrange("p (j k) -> p j k", j=4)
+            for i in range(pieces):
+                nc.sync.dma_start(
+                    out=w_sb[:, :, wid * i:wid * i + wid],
+                    in_=w_qkv[r0:r0 + 512, wid * i:wid * i + wid].rearrange("(j p) k -> p j k", j=4))
+
+        if LAYOUT == "perm":
+            wmove = const.tile([P, P], F32)
+            nc.vector.tensor_copy(out=wmove[:].rearrange("p (e i) -> p e i", e=2),
+                                  in_=ident[:].rearrange("p (i e) -> p e i", e=2))
+        else:
+            wmove = ident
 
         xf = xraw[:].bitcast(F32)
         xgrp = const.tile([P, 4096], BF16, align_bytes=64)
@@ -99,34 +109,43 @@ def tile_attention_pa_kernel(tc, hidden_states, cos, sin, w_qkv, out_0, out_1, o
 
         cosd = const.tile([P, P], F32)
         sind = const.tile([P, P], F32)
-        nc.vector.tensor_copy(out=cosd[:].rearrange("p (e i) -> p e i", e=2),
-                              in_=cos_raw[:].rearrange("p (i e) -> p e i", e=2))
-        sin_v = sin_raw[:].rearrange("p (i e) -> p e i", e=2)
-        nc.vector.tensor_scalar_mul(out=sind[:, 0:64], in0=sin_v[:, 0, :], scalar1=-1.0)
-        nc.vector.tensor_copy(out=sind[:, 64:128], in_=sin_v[:, 1, :])
+        if LAYOUT == "perm":
+            nc.vector.tensor_copy(out=cosd[:].rearrange("p (e i) -> p e i", e=2),
+                                  in_=cos_raw[:].rearrange("p (i e) -> p e i", e=2))
+            sin_v = sin_raw[:].rearrange("p (i e) -> p e i", e=2)
+            nc.vector.tensor_scalar_mul(out=sind[:, 0:64], in0=sin_v[:, 0, :], scalar1=-1.0)
+            nc.vector.tensor_copy(out=sind[:, 64:128], in_=sin_v[:, 1, :])
+        else:
+            nc.vector.tensor_copy(out=cosd[:], in_=cos_raw[:])
+            sin_v = sin_raw[:].rearrange("p (i e) -> p i e", e=2)
+            sind_v = sind[:].rearrange("p (i e) -> p i e", e=2)
+            nc.vector.tensor_scalar_mul(out=sind_v[:, :, 0], in0=sin_v[:, :, 0], scalar1=-1.0)
+            nc.vector.tensor_copy(out=sind_v[:, :, 1], in_=sin_v[:, :, 1])
 
         grps = {}
         codes = {}
         accs = {}
 
-        def transposes(c):
+        def transposes(c, half):
             wf = wraws[c][:].bitcast(F32)
-            for half in range(2):
-                grp = gpool.tile([P, 4096], BF16, align_bytes=64, tag="grp")
-                grps[(c, half)] = grp
-                gf = grp[:].bitcast(F32)
-                for gg in range(2):
-                    g = 2 * half + gg
-                    for e in range(2):
-                        tp = psum_t.tile([P, 512], F32, tag="tp")
-                        for t in range(4):
-                            j = 2 * (t // 2) + e
-                            u = t % 2
-                            o = 1024 * j + 256 * g + 128 * u
-                            nc.tensor.transpose(tp[:, 128 * t:128 * t + 128], wf[:, o:o + 128], ident[:])
-                        dst = gf[:, 1024 * gg:1024 * gg + 1024].rearrange(
-                            "q (h e r) -> q h e r", h=4, e=2)[:, :, e, :].rearrange("q h (pp t) -> q h pp t", t=4)
-                        src = tp[:].rearrange("q (t h pp) -> q h pp t", t=4, h=4)
+            grp = gpool.tile([P, 4096], BF16, align_bytes=64, tag="grp")
+            grps[(c, half)] = grp
+            gf = grp[:].bitcast(F32)
+            for gg in range(2):
+                g = 2 * half + gg
+                for jp in range(2):
+                    tp = psum_t.tile([P, 512], F32, tag="tp")
+                    for t in range(4):
+                        j = 2 * jp + t // 2
+                        u = t % 2
+                        o = 1024 * j + 256 * g + 128 * u
+                        nc.tensor.transpose(tp[:, 128 * t:128 * t + 128], wf[:, o:o + 128], wmove[:])
+                    lo = 1024 * gg + 512 * jp
+                    dst = gf[:, lo:lo + 512].rearrange("q (j c u) -> q j c u", j=2, u=2)
+                    src = tp[:].rearrange("q (j u c) -> q j c u", j=2, u=2)
+                    if (2 * g + jp) in VCOPY:
+                        nc.vector.tensor_copy(out=dst, in_=src)
+                    else:
                         nc.scalar.copy(out=dst, in_=src)
 
         def quantise(c, half):
@@ -136,6 +155,9 @@ def tile_attention_pa_kernel(tc, hidden_states, cos, sin, w_qkv, out_0, out_1, o
             nc.vector.quantize_mx(out=wc[:].bitcast(FP8X4), scales=ws[:], in_=grps[(c, half)][:])
 
         def mx_pass(c, g, b):
+            if g == 0:
+                acc = psum_a.tile([P, 512], F32, tag="acc")
+                accs[(c, b)] = acc
             wc, ws = codes[(c, g // 2)]
             lo = 512 * (g % 2)
             xo = 256 * g + 128 * b
@@ -143,19 +165,6 @@ def tile_attention_pa_kernel(tc, hidden_states, cos, sin, w_qkv, out_0, out_1, o
                                 lhsT=xc[:, xo:xo + 128].bitcast(FP8X4), lhsT_scale=xs[:, xo:xo + 128],
                                 rhs=wc[:, lo:lo + 512].bitcast(FP8X4), rhs_scale=ws[:, lo:lo + 512],
                                 start=(g == 0), stop=(g == 3))
-
-        def matmuls(c, g_major):
-            for b in range(2):
-                acc = psum_a.tile([P, 512], F32, tag="acc")
-                accs[(c, b)] = acc
-            if g_major:
-                for g in range(4):
-                    for b in range(2):
-                        mx_pass(c, g, b)
-            else:
-                for b in range(2):
-                    for g in range(4):
-                        mx_pass(c, g, b)
 
         rope_t = {}
 
@@ -167,22 +176,37 @@ def tile_attention_pa_kernel(tc, hidden_states, cos, sin, w_qkv, out_0, out_1, o
             nc.vector.tensor_tensor(out=t1[:].rearrange("p (h m) -> p h m", h=4),
                                     in0=acc[:].rearrange("p (h m) -> p h m", h=4),
                                     in1=cosd[:].unsqueeze(1).to_broadcast([P, 4, P]), op=MULT)
-            a4 = acc[:].rearrange("p (h e i) -> p h e i", h=4, e=2)
-            t4 = t2[:].rearrange("p (h e i) -> p h e i", h=4, e=2)
-            for e in range(2):
-                nc.vector.tensor_tensor(out=t4[:, :, e, :], in0=a4[:, :, 1 - e, :],
-                                        in1=sind[:, 64 * e:64 * e + 64].unsqueeze(1).to_broadcast([P, 4, 64]),
-                                        op=MULT)
+            if LAYOUT == "perm":
+                a4 = acc[:].rearrange("p (h e i) -> p h e i", h=4, e=2)
+                t4 = t2[:].rearrange("p (h e i) -> p h e i", h=4, e=2)
+                for e in range(2):
+                    nc.vector.tensor_tensor(out=t4[:, :, e, :], in0=a4[:, :, 1 - e, :],
+                                            in1=sind[:, 64 * e:64 * e + 64].unsqueeze(1).to_broadcast([P, 4, 64]),
+                                            op=MULT)
+            else:
+                nc.vector.tensor_tensor(
+                    out=t2[:].rearrange("p (h i e) -> p h i e", h=4, e=2),
+                    in0=acc[:].rearrange("p (h i e) -> p h i e", h=4, e=2)[:, :, :, ::-1],
+                    in1=sind[:].rearrange("p (i e) -> p i e", e=2).unsqueeze(1).to_broadcast([P, 4, 64, 2]),
+                    op=MULT)
 
         def rope_add(c, b, ost):
             t1, t2 = rope_t[(c, b)]
-            nc.vector.tensor_tensor(out=ost[:, 512 * b:512 * b + 512].rearrange("p (h i e) -> p h i e", h=4, e=2),
-                                    in0=t1[:].rearrange("p (h e i) -> p h i e", h=4, e=2),
-                                    in1=t2[:].rearrange("p (h e i) -> p h i e", h=4, e=2), op=ADD)
+            eng = nc.gpsimd if GADD else nc.vector
+            if LAYOUT == "perm":
+                eng.tensor_tensor(out=ost[:, 512 * b:512 * b + 512].rearrange("p (h i e) -> p h i e", h=4, e=2),
+                                  in0=t1[:].rearrange("p (h e i) -> p h i e", h=4, e=2),
+                                  in1=t2[:].rearrange("p (h e i) -> p h i e", h=4, e=2), op=ADD)
+            else:
+                eng.tensor_tensor(out=ost[:, 512 * b:512 * b + 512], in0=t1[:], in1=t2[:], op=ADD)
 
         def plain_out(c, b, ost, eng):
-            dst = ost[:, 512 * b:512 * b + 512].rearrange("p (h i e) -> p h i e", h=4, e=2)
-            src = accs[(c, b)][:].rearrange("p (h e i) -> p h i e", h=4, e=2)
+            if LAYOUT == "perm":
+                dst = ost[:, 512 * b:512 * b + 512].rearrange("p (h i e) -> p h i e", h=4, e=2)
+                src = accs[(c, b)][:].rearrange("p (h e i) -> p h i e", h=4, e=2)
+            else:
+                dst = ost[:, 512 * b:512 * b + 512]
+                src = accs[(c, b)][:]
             if eng == "s":
                 nc.scalar.copy(out=dst, in_=src)
             else:
@@ -196,10 +220,28 @@ def tile_attention_pa_kernel(tc, hidden_states, cos, sin, w_qkv, out_0, out_1, o
 
         for c in range(NCHUNK + 1):
             d = c - 1
-            if c < NCHUNK:
-                transposes(c)
+            last = d == NCHUNK - 1
+            if HALF:
+                for half in range(2):
+                    if c < NCHUNK:
+                        transposes(c, half)
+                    if d >= 0:
+                        for g in (2 * half, 2 * half + 1):
+                            for b in range(2):
+                                mx_pass(d, g, b)
+            else:
+                if c < NCHUNK:
+                    transposes(c, 0)
+                    transposes(c, 1)
+                if last:
+                    for g in range(4):
+                        for b in range(2):
+                            mx_pass(d, g, b)
+                elif d >= 0:
+                    for b in range(2):
+                        for g in range(4):
+                            mx_pass(d, g, b)
             if d >= 0:
-                matmuls(d, g_major=(d == NCHUNK - 1))
                 ost = opool.tile([P, 1024], F32, tag="ost")
             roped = d >= 0 and order[d][0] < 2
             if c < NCHUNK:
@@ -214,6 +256,6 @@ def tile_attention_pa_kernel(tc, hidden_states, cos, sin, w_qkv, out_0, out_1, o
                 rope_add(d, 1, ost)
             elif d >= 0:
                 plain_out(d, 0, ost, "s")
-                plain_out(d, 1, ost, "v")
+                plain_out(d, 1, ost, "s" if (last and LAST_S) else "v")
             if d >= 0:
                 store(d, ost)

@@ -19,13 +19,13 @@ W_BUFS = 6
 GRP_BUFS = 4
 CODE_BUFS = 4
 OST_BUFS = 10
-T_BANKS = 5
-A_BANKS = 3
+T_BANKS = 4
+A_BANKS = 4
 R_BUFS = 2
 STORE_Q = "sync"
 PIN = True
 LAYOUT = "nat"
-HALF = False
+HALF = True
 VCOPY = ()
 LAST_S = False
 GADD = False

@@ -14,27 +14,29 @@ ADD = mybir.AluOpType.add
 FLOPS = 2 * 256 * 6144 * 2048
 
 P = 128
-NCHUNK = 12
-W_BUFS = 6
+NUNIT = 24
+W_BUFS = 12
 GRP_BUFS = 4
 CODE_BUFS = 4
 OST_BUFS = 10
 T_BANKS = 4
 A_BANKS = 4
 R_BUFS = 2
-STORE_Q = "sync"
-PIN = True
-LAYOUT = "nat"
-HALF = True
-VCOPY = ()
-LAST_S = False
+PATTERN = "RRRVRRRVRRVV"
 GADD = False
+PLAIN_ENG = "v"
+LAG = 2
+STORE_Q = "sync"
 
 
 def tile_attention_pa_kernel(tc, hidden_states, cos, sin, w_qkv, out_0, out_1, out_2):
     nc = tc.nc
     outs = (out_0, out_1, out_2)
-    order = [(kind, hc) for hc in range(4) for kind in range(3)]
+    rotated = [(kind, hc) for hc in range(4) for kind in range(2)]
+    plain = [(2, hc) for hc in range(4)]
+    groups = []
+    for ch in PATTERN:
+        groups.append(rotated.pop(0) if ch == "R" else plain.pop(0))
     with ExitStack() as ctx:
         const = ctx.enter_context(tc.tile_pool(name="const", bufs=1))
         wpool = ctx.enter_context(tc.tile_pool(name="wpool", bufs=W_BUFS))
@@ -44,9 +46,7 @@ def tile_attention_pa_kernel(tc, hidden_states, cos, sin, w_qkv, out_0, out_1, o
         opool = ctx.enter_context(tc.tile_pool(name="opool", bufs=OST_BUFS))
         psum_t = ctx.enter_context(tc.psum_pool(name="psum_t", bufs=T_BANKS))
         psum_a = ctx.enter_context(tc.psum_pool(name="psum_a", bufs=A_BANKS))
-        if PIN:
-            ctx.enter_context(tc.manual_schedule())
-
+        ctx.enter_context(tc.manual_schedule())
         store_eng = {"sync": nc.sync, "gpsimd": nc.gpsimd, "scalar": nc.scalar}[STORE_Q]
 
         ident = const.tile([P, P], F32)
@@ -64,25 +64,13 @@ def tile_attention_pa_kernel(tc, hidden_states, cos, sin, w_qkv, out_0, out_1, o
                               in_=x_dram[:, :, 1024 * hf:1024 * hf + 1024])
 
         wraws = []
-        for c in range(NCHUNK):
-            kind, hc = order[c]
-            r0 = 2048 * kind + 512 * hc
-            wraw = wpool.tile([P, 8192], BF16)
+        for u in range(NUNIT):
+            kind, hc = groups[u // 2]
+            r0 = 2048 * kind + 512 * hc + 256 * (u % 2)
+            wraw = wpool.tile([P, 4096], BF16)
             wraws.append(wraw)
-            pieces = 4 if c == 0 else (2 if c == 1 else 1)
-            wid = 2048 // pieces
-            w_sb = wraw[:].rearrange("p (j k) -> p j k", j=4)
-            for i in range(pieces):
-                nc.sync.dma_start(
-                    out=w_sb[:, :, wid * i:wid * i + wid],
-                    in_=w_qkv[r0:r0 + 512, wid * i:wid * i + wid].rearrange("(j p) k -> p j k", j=4))
-
-        if LAYOUT == "perm":
-            wmove = const.tile([P, P], F32)
-            nc.vector.tensor_copy(out=wmove[:].rearrange("p (e i) -> p e i", e=2),
-                                  in_=ident[:].rearrange("p (i e) -> p e i", e=2))
-        else:
-            wmove = ident
+            nc.sync.dma_start(out=wraw[:].rearrange("p (j k) -> p j k", j=2),
+                              in_=w_qkv[r0:r0 + 256, :].rearrange("(j p) k -> p j k", j=2))
 
         xf = xraw[:].bitcast(F32)
         xgrp = const.tile([P, 4096], BF16, align_bytes=64)
@@ -92,10 +80,8 @@ def tile_attention_pa_kernel(tc, hidden_states, cos, sin, w_qkv, out_0, out_1, o
         for g in range(4):
             tpx = psum_t.tile([P, 512], F32, tag="tp")
             for t in range(4):
-                b, u = t // 2, t % 2
-                nc.tensor.transpose(tpx[:, 128 * t:128 * t + 128],
-                                    xf[:, 1024 * b + 256 * g + 128 * u:1024 * b + 256 * g + 128 * u + 128],
-                                    ident[:])
+                o = 1024 * (t // 2) + 256 * g + 128 * (t % 2)
+                nc.tensor.transpose(tpx[:, 128 * t:128 * t + 128], xf[:, o:o + 128], ident[:])
             dst = xgf[:, 512 * g:512 * g + 512].rearrange("q (b s u) -> q b s u", b=2, u=2)
             src = tpx[:].rearrange("q (b u s) -> q b s u", b=2, u=2)
             if g % 2 == 0:
@@ -109,153 +95,96 @@ def tile_attention_pa_kernel(tc, hidden_states, cos, sin, w_qkv, out_0, out_1, o
 
         cosd = const.tile([P, P], F32)
         sind = const.tile([P, P], F32)
-        if LAYOUT == "perm":
-            nc.vector.tensor_copy(out=cosd[:].rearrange("p (e i) -> p e i", e=2),
-                                  in_=cos_raw[:].rearrange("p (i e) -> p e i", e=2))
-            sin_v = sin_raw[:].rearrange("p (i e) -> p e i", e=2)
-            nc.vector.tensor_scalar_mul(out=sind[:, 0:64], in0=sin_v[:, 0, :], scalar1=-1.0)
-            nc.vector.tensor_copy(out=sind[:, 64:128], in_=sin_v[:, 1, :])
-        else:
-            nc.vector.tensor_copy(out=cosd[:], in_=cos_raw[:])
-            sin_v = sin_raw[:].rearrange("p (i e) -> p i e", e=2)
-            sind_v = sind[:].rearrange("p (i e) -> p i e", e=2)
-            nc.vector.tensor_scalar_mul(out=sind_v[:, :, 0], in0=sin_v[:, :, 0], scalar1=-1.0)
-            nc.vector.tensor_copy(out=sind_v[:, :, 1], in_=sin_v[:, :, 1])
+        nc.vector.tensor_copy(out=cosd[:], in_=cos_raw[:])
+        sin_v = sin_raw[:].rearrange("p (i e) -> p i e", e=2)
+        sind_v = sind[:].rearrange("p (i e) -> p i e", e=2)
+        nc.vector.tensor_scalar_mul(out=sind_v[:, :, 0], in0=sin_v[:, :, 0], scalar1=-1.0)
+        nc.vector.tensor_copy(out=sind_v[:, :, 1], in_=sin_v[:, :, 1])
 
         grps = {}
         codes = {}
         accs = {}
+        osts = {}
 
-        def transposes(c, half):
-            wf = wraws[c][:].bitcast(F32)
+        def transposes(u):
+            wf = wraws[u][:].bitcast(F32)
             grp = gpool.tile([P, 4096], BF16, align_bytes=64, tag="grp")
-            grps[(c, half)] = grp
+            grps[u] = grp
             gf = grp[:].bitcast(F32)
-            for gg in range(2):
-                g = 2 * half + gg
-                for jp in range(2):
-                    tp = psum_t.tile([P, 512], F32, tag="tp")
-                    for t in range(4):
-                        j = 2 * jp + t // 2
-                        u = t % 2
-                        o = 1024 * j + 256 * g + 128 * u
-                        nc.tensor.transpose(tp[:, 128 * t:128 * t + 128], wf[:, o:o + 128], wmove[:])
-                    lo = 1024 * gg + 512 * jp
-                    dst = gf[:, lo:lo + 512].rearrange("q (j c u) -> q j c u", j=2, u=2)
-                    src = tp[:].rearrange("q (j u c) -> q j c u", j=2, u=2)
-                    if (2 * g + jp) in VCOPY:
-                        nc.vector.tensor_copy(out=dst, in_=src)
-                    else:
-                        nc.scalar.copy(out=dst, in_=src)
+            for g in range(4):
+                tp = psum_t.tile([P, 512], F32, tag="tp")
+                for t in range(4):
+                    o = 1024 * (t // 2) + 256 * g + 128 * (t % 2)
+                    nc.tensor.transpose(tp[:, 128 * t:128 * t + 128], wf[:, o:o + 128], ident[:])
+                nc.scalar.copy(out=gf[:, 512 * g:512 * g + 512].rearrange("q (j c u) -> q j c u", j=2, u=2),
+                               in_=tp[:].rearrange("q (j u c) -> q j c u", j=2, u=2))
 
-        def quantise(c, half):
+        def quantise(u):
             wc = cpool.tile([P, 1024], U32, align_bytes=64, tag="wc")
             ws = cpool.tile([P, 1024], U8, align_bytes=64, tag="ws")
-            codes[(c, half)] = (wc, ws)
-            nc.vector.quantize_mx(out=wc[:].bitcast(FP8X4), scales=ws[:], in_=grps[(c, half)][:])
+            codes[u] = (wc, ws)
+            pieces = 4 if u == NUNIT - 1 else 1
+            n = 1024 // pieces
+            for i in range(pieces):
+                nc.vector.quantize_mx(out=wc[:, n * i:n * i + n].bitcast(FP8X4), scales=ws[:, n * i:n * i + n],
+                                      in_=grps[u][:, 4 * n * i:4 * n * i + 4 * n])
 
-        def mx_pass(c, g, b):
-            if g == 0:
-                acc = psum_a.tile([P, 512], F32, tag="acc")
-                accs[(c, b)] = acc
-            wc, ws = codes[(c, g // 2)]
-            lo = 512 * (g % 2)
-            xo = 256 * g + 128 * b
-            nc.tensor.matmul_mx(out=accs[(c, b)][:],
-                                lhsT=xc[:, xo:xo + 128].bitcast(FP8X4), lhsT_scale=xs[:, xo:xo + 128],
-                                rhs=wc[:, lo:lo + 512].bitcast(FP8X4), rhs_scale=ws[:, lo:lo + 512],
-                                start=(g == 0), stop=(g == 3))
+        def matmuls(u):
+            acc = psum_a.tile([P, 512], F32, tag="acc")
+            accs[u] = acc
+            wc, ws = codes[u]
+            for b in range(2):
+                for g in range(4):
+                    xo = 256 * g + 128 * b
+                    nc.tensor.matmul_mx(out=acc[:, 256 * b:256 * b + 256],
+                                        lhsT=xc[:, xo:xo + 128].bitcast(FP8X4), lhsT_scale=xs[:, xo:xo + 128],
+                                        rhs=wc[:, 256 * g:256 * g + 256].bitcast(FP8X4),
+                                        rhs_scale=ws[:, 256 * g:256 * g + 256],
+                                        start=(g == 0), stop=(g == 3))
 
-        rope_t = {}
-
-        def rope_mults(c, b):
-            acc = accs[(c, b)]
-            t1 = rpool.tile([P, 512], F32, tag="t1")
-            t2 = rpool.tile([P, 512], F32, tag="t2")
-            rope_t[(c, b)] = (t1, t2)
-            nc.vector.tensor_tensor(out=t1[:].rearrange("p (h m) -> p h m", h=4),
-                                    in0=acc[:].rearrange("p (h m) -> p h m", h=4),
-                                    in1=cosd[:].unsqueeze(1).to_broadcast([P, 4, P]), op=MULT)
-            if LAYOUT == "perm":
-                a4 = acc[:].rearrange("p (h e i) -> p h e i", h=4, e=2)
-                t4 = t2[:].rearrange("p (h e i) -> p h e i", h=4, e=2)
-                for e in range(2):
-                    nc.vector.tensor_tensor(out=t4[:, :, e, :], in0=a4[:, :, 1 - e, :],
-                                            in1=sind[:, 64 * e:64 * e + 64].unsqueeze(1).to_broadcast([P, 4, 64]),
-                                            op=MULT)
-            else:
+        def finish(u):
+            kind, hc = groups[u // 2]
+            jp = u % 2
+            acc = accs[u]
+            if jp == 0:
+                ost = opool.tile([P, 1024], F32, tag="ost")
+                osts[u // 2] = ost
+            ost = osts[u // 2]
+            dst = ost[:].rearrange("p (b m) -> p b m", b=2)[:, :, 256 * jp:256 * jp + 256]
+            if kind < 2:
+                t1 = rpool.tile([P, 512], F32, tag="t1")
+                t2 = rpool.tile([P, 512], F32, tag="t2")
+                nc.vector.tensor_tensor(out=t1[:].rearrange("p (h m) -> p h m", h=4),
+                                        in0=acc[:].rearrange("p (h m) -> p h m", h=4),
+                                        in1=cosd[:].unsqueeze(1).to_broadcast([P, 4, P]), op=MULT)
                 nc.vector.tensor_tensor(
                     out=t2[:].rearrange("p (h i e) -> p h i e", h=4, e=2),
                     in0=acc[:].rearrange("p (h i e) -> p h i e", h=4, e=2)[:, :, :, ::-1],
                     in1=sind[:].rearrange("p (i e) -> p i e", e=2).unsqueeze(1).to_broadcast([P, 4, 64, 2]),
                     op=MULT)
-
-        def rope_add(c, b, ost):
-            t1, t2 = rope_t[(c, b)]
-            eng = nc.gpsimd if GADD else nc.vector
-            if LAYOUT == "perm":
-                eng.tensor_tensor(out=ost[:, 512 * b:512 * b + 512].rearrange("p (h i e) -> p h i e", h=4, e=2),
-                                  in0=t1[:].rearrange("p (h e i) -> p h i e", h=4, e=2),
-                                  in1=t2[:].rearrange("p (h e i) -> p h i e", h=4, e=2), op=ADD)
+                add_eng = nc.gpsimd if GADD else nc.vector
+                add_eng.tensor_tensor(out=dst, in0=t1[:].rearrange("p (b m) -> p b m", b=2),
+                                      in1=t2[:].rearrange("p (b m) -> p b m", b=2), op=ADD)
             else:
-                eng.tensor_tensor(out=ost[:, 512 * b:512 * b + 512], in0=t1[:], in1=t2[:], op=ADD)
+                src = acc[:].rearrange("p (b m) -> p b m", b=2)
+                if PLAIN_ENG == "s" or u >= NUNIT - 2:
+                    nc.scalar.copy(out=dst, in_=src)
+                else:
+                    nc.vector.tensor_copy(out=dst, in_=src)
+            o_dram = outs[kind].rearrange("b s h l -> s b (h l)")
+            if u // 2 == NUNIT // 2 - 1:
+                lo = 512 * hc + 256 * jp
+                store_eng.dma_start(out=o_dram[:, :, lo:lo + 256], in_=dst)
+            elif jp == 1:
+                store_eng.dma_start(out=o_dram[:, :, 512 * hc:512 * hc + 512],
+                                    in_=ost[:].rearrange("p (b m) -> p b m", b=2))
 
-        def plain_out(c, b, ost, eng):
-            if LAYOUT == "perm":
-                dst = ost[:, 512 * b:512 * b + 512].rearrange("p (h i e) -> p h i e", h=4, e=2)
-                src = accs[(c, b)][:].rearrange("p (h e i) -> p h i e", h=4, e=2)
-            else:
-                dst = ost[:, 512 * b:512 * b + 512]
-                src = accs[(c, b)][:]
-            if eng == "s":
-                nc.scalar.copy(out=dst, in_=src)
-            else:
-                nc.vector.tensor_copy(out=dst, in_=src)
-
-        def store(c, ost):
-            kind, hc = order[c]
-            store_eng.dma_start(
-                out=outs[kind].rearrange("b s h l -> s b (h l)")[:, :, 512 * hc:512 * hc + 512],
-                in_=ost[:].rearrange("p (b m) -> p b m", b=2))
-
-        for c in range(NCHUNK + 1):
-            d = c - 1
-            last = d == NCHUNK - 1
-            if HALF:
-                for half in range(2):
-                    if c < NCHUNK:
-                        transposes(c, half)
-                    if d >= 0:
-                        for g in (2 * half, 2 * half + 1):
-                            for b in range(2):
-                                mx_pass(d, g, b)
-            else:
-                if c < NCHUNK:
-                    transposes(c, 0)
-                    transposes(c, 1)
-                if last:
-                    for g in range(4):
-                        for b in range(2):
-                            mx_pass(d, g, b)
-                elif d >= 0:
-                    for b in range(2):
-                        for g in range(4):
-                            mx_pass(d, g, b)
-            if d >= 0:
-                ost = opool.tile([P, 1024], F32, tag="ost")
-            roped = d >= 0 and order[d][0] < 2
-            if c < NCHUNK:
-                quantise(c, 0)
-            if roped:
-                rope_mults(d, 0)
-            if c < NCHUNK:
-                quantise(c, 1)
-            if roped:
-                rope_mults(d, 1)
-                rope_add(d, 0, ost)
-                rope_add(d, 1, ost)
-            elif d >= 0:
-                plain_out(d, 0, ost, "s")
-                plain_out(d, 1, ost, "s" if (last and LAST_S) else "v")
-            if d >= 0:
-                store(d, ost)
+        for u in range(NUNIT + LAG):
+            if u < NUNIT:
+                transposes(u)
+            if u >= LAG:
+                matmuls(u - LAG)
+            if u < NUNIT:
+                quantise(u)
+            if u >= LAG:
+                finish(u - LAG)

@@ -21,9 +21,9 @@ CODE_BUFS = 4
 OST_BUFS = 10
 T_BANKS = 4
 A_BANKS = 4
-R_BUFS = 2
+R_BUFS = 3
 PATTERN = "RRRVRRRVRRVV"
-GADD = False
+GADD = True
 PLAIN_ENG = "v"
 LAG = 2
 STORE_Q = "sync"

@@ -19,14 +19,16 @@ W_BUFS = 12
 GRP_BUFS = 4
 CODE_BUFS = 4
 OST_BUFS = 10
-T_BANKS = 4
-A_BANKS = 4
+T_BANKS = 5
+A_BANKS = 3
 R_BUFS = 3
 PATTERN = "RRRVRRRVRRVV"
 GADD = True
 PLAIN_ENG = "v"
 LAG = 2
 STORE_Q = "sync"
+TAIL_S = 4
+SPLIT_LAST = True
 
 
 def tile_attention_pa_kernel(tc, hidden_states, cos, sin, w_qkv, out_0, out_1, out_2):
@@ -105,6 +107,7 @@ def tile_attention_pa_kernel(tc, hidden_states, cos, sin, w_qkv, out_0, out_1, o
         codes = {}
         accs = {}
         osts = {}
+        accs_b = {}
 
         def transposes(u):
             wf = wraws[u][:].bitcast(F32)
@@ -130,13 +133,19 @@ def tile_attention_pa_kernel(tc, hidden_states, cos, sin, w_qkv, out_0, out_1, o
                                       in_=grps[u][:, 4 * n * i:4 * n * i + 4 * n])
 
         def matmuls(u):
+            split = SPLIT_LAST and u == NUNIT - 1
             acc = psum_a.tile([P, 512], F32, tag="acc")
+            acc_b = [acc[:, 0:256], acc[:, 256:512]]
+            if split:
+                acc2 = psum_a.tile([P, 512], F32, tag="acc")
+                acc_b = [acc[:, 0:256], acc2[:, 0:256]]
             accs[u] = acc
+            accs_b[u] = acc_b
             wc, ws = codes[u]
             for b in range(2):
                 for g in range(4):
                     xo = 256 * g + 128 * b
-                    nc.tensor.matmul_mx(out=acc[:, 256 * b:256 * b + 256],
+                    nc.tensor.matmul_mx(out=acc_b[b],
                                         lhsT=xc[:, xo:xo + 128].bitcast(FP8X4), lhsT_scale=xs[:, xo:xo + 128],
                                         rhs=wc[:, 256 * g:256 * g + 256].bitcast(FP8X4),
                                         rhs_scale=ws[:, 256 * g:256 * g + 256],
@@ -151,6 +160,14 @@ def tile_attention_pa_kernel(tc, hidden_states, cos, sin, w_qkv, out_0, out_1, o
                 osts[u // 2] = ost
             ost = osts[u // 2]
             dst = ost[:].rearrange("p (b m) -> p b m", b=2)[:, :, 256 * jp:256 * jp + 256]
+            o_dram = outs[kind].rearrange("b s h l -> s b (h l)")
+            if SPLIT_LAST and u == NUNIT - 1:
+                lo = 512 * hc + 256 * jp
+                for b in range(2):
+                    nc.scalar.copy(out=ost[:, 512 * b + 256 * jp:512 * b + 256 * jp + 256], in_=accs_b[u][b])
+                    store_eng.dma_start(out=o_dram[:, b, lo:lo + 256],
+                                        in_=ost[:, 512 * b + 256 * jp:512 * b + 256 * jp + 256])
+                return
             if kind < 2:
                 t1 = rpool.tile([P, 512], F32, tag="t1")
                 t2 = rpool.tile([P, 512], F32, tag="t2")
@@ -167,11 +184,10 @@ def tile_attention_pa_kernel(tc, hidden_states, cos, sin, w_qkv, out_0, out_1, o
                                       in1=t2[:].rearrange("p (b m) -> p b m", b=2), op=ADD)
             else:
                 src = acc[:].rearrange("p (b m) -> p b m", b=2)
-                if PLAIN_ENG == "s" or u >= NUNIT - 2:
+                if PLAIN_ENG == "s" or u >= NUNIT - TAIL_S:
                     nc.scalar.copy(out=dst, in_=src)
                 else:
                     nc.vector.tensor_copy(out=dst, in_=src)
-            o_dram = outs[kind].rearrange("b s h l -> s b (h l)")
             if u // 2 == NUNIT // 2 - 1:
                 lo = 512 * hc + 256 * jp
                 store_eng.dma_start(out=o_dram[:, :, lo:lo + 256], in_=dst)

@@ -19,16 +19,16 @@ W_BUFS = 12
 GRP_BUFS = 4
 CODE_BUFS = 4
 OST_BUFS = 10
-T_BANKS = 5
-A_BANKS = 3
+T_BANKS = 4
+A_BANKS = 4
 R_BUFS = 3
 PATTERN = "RRRVRRRVRRVV"
 GADD = True
 PLAIN_ENG = "v"
 LAG = 2
 STORE_Q = "sync"
-TAIL_S = 4
-SPLIT_LAST = True
+WARM_FIRST = 6
+WARM_NEXT = 3
 
 
 def tile_attention_pa_kernel(tc, hidden_states, cos, sin, w_qkv, out_0, out_1, out_2):
@@ -50,6 +50,14 @@ def tile_attention_pa_kernel(tc, hidden_states, cos, sin, w_qkv, out_0, out_1, o
         psum_a = ctx.enter_context(tc.psum_pool(name="psum_a", bufs=A_BANKS))
         ctx.enter_context(tc.manual_schedule())
         store_eng = {"sync": nc.sync, "gpsimd": nc.gpsimd, "scalar": nc.scalar}[STORE_Q]
+
+        warm_sb = const.tile([P, 512], BF16)
+        nc.vector.memset(warm_sb[:], 0.0)
+        warm_ps = psum_a.tile([P, 512], F32, tag="acc")
+
+        def keep_clock(n):
+            for i in range(n):
+                nc.tensor.matmul(out=warm_ps[:], lhsT=warm_sb[:, 0:P], rhs=warm_sb[:], start=True, stop=True)
 
         ident = const.tile([P, P], F32)
         make_identity(nc, ident[:])
@@ -79,6 +87,7 @@ def tile_attention_pa_kernel(tc, hidden_states, cos, sin, w_qkv, out_0, out_1, o
         xgf = xgrp[:].bitcast(F32)
         xc = const.tile([P, 1024], U32, align_bytes=64)
         xs = const.tile([P, 1024], U8, align_bytes=64)
+        keep_clock(WARM_FIRST)
         for g in range(4):
             tpx = psum_t.tile([P, 512], F32, tag="tp")
             for t in range(4):
@@ -90,6 +99,7 @@ def tile_attention_pa_kernel(tc, hidden_states, cos, sin, w_qkv, out_0, out_1, o
                 nc.scalar.copy(out=dst, in_=src)
             else:
                 nc.vector.tensor_copy(out=dst, in_=src)
+        keep_clock(WARM_NEXT)
         for hf in range(2):
             nc.vector.quantize_mx(out=xc[:, 512 * hf:512 * hf + 512].bitcast(FP8X4),
                                   scales=xs[:, 512 * hf:512 * hf + 512],
@@ -107,7 +117,6 @@ def tile_attention_pa_kernel(tc, hidden_states, cos, sin, w_qkv, out_0, out_1, o
         codes = {}
         accs = {}
         osts = {}
-        accs_b = {}
 
         def transposes(u):
             wf = wraws[u][:].bitcast(F32)
@@ -133,19 +142,13 @@ def tile_attention_pa_kernel(tc, hidden_states, cos, sin, w_qkv, out_0, out_1, o
                                       in_=grps[u][:, 4 * n * i:4 * n * i + 4 * n])
 
         def matmuls(u):
-            split = SPLIT_LAST and u == NUNIT - 1
             acc = psum_a.tile([P, 512], F32, tag="acc")
-            acc_b = [acc[:, 0:256], acc[:, 256:512]]
-            if split:
-                acc2 = psum_a.tile([P, 512], F32, tag="acc")
-                acc_b = [acc[:, 0:256], acc2[:, 0:256]]
             accs[u] = acc
-            accs_b[u] = acc_b
             wc, ws = codes[u]
             for b in range(2):
                 for g in range(4):
                     xo = 256 * g + 128 * b
-                    nc.tensor.matmul_mx(out=acc_b[b],
+                    nc.tensor.matmul_mx(out=acc[:, 256 * b:256 * b + 256],
                                         lhsT=xc[:, xo:xo + 128].bitcast(FP8X4), lhsT_scale=xs[:, xo:xo + 128],
                                         rhs=wc[:, 256 * g:256 * g + 256].bitcast(FP8X4),
                                         rhs_scale=ws[:, 256 * g:256 * g + 256],
@@ -160,14 +163,6 @@ def tile_attention_pa_kernel(tc, hidden_states, cos, sin, w_qkv, out_0, out_1, o
                 osts[u // 2] = ost
             ost = osts[u // 2]
             dst = ost[:].rearrange("p (b m) -> p b m", b=2)[:, :, 256 * jp:256 * jp + 256]
-            o_dram = outs[kind].rearrange("b s h l -> s b (h l)")
-            if SPLIT_LAST and u == NUNIT - 1:
-                lo = 512 * hc + 256 * jp
-                for b in range(2):
-                    nc.scalar.copy(out=ost[:, 512 * b + 256 * jp:512 * b + 256 * jp + 256], in_=accs_b[u][b])
-                    store_eng.dma_start(out=o_dram[:, b, lo:lo + 256],
-                                        in_=ost[:, 512 * b + 256 * jp:512 * b + 256 * jp + 256])
-                return
             if kind < 2:
                 t1 = rpool.tile([P, 512], F32, tag="t1")
                 t2 = rpool.tile([P, 512], F32, tag="t2")
@@ -184,10 +179,11 @@ def tile_attention_pa_kernel(tc, hidden_states, cos, sin, w_qkv, out_0, out_1, o
                                       in1=t2[:].rearrange("p (b m) -> p b m", b=2), op=ADD)
             else:
                 src = acc[:].rearrange("p (b m) -> p b m", b=2)
-                if PLAIN_ENG == "s" or u >= NUNIT - TAIL_S:
+                if PLAIN_ENG == "s" or u >= NUNIT - 2:
                     nc.scalar.copy(out=dst, in_=src)
                 else:
                     nc.vector.tensor_copy(out=dst, in_=src)
+            o_dram = outs[kind].rearrange("b s h l -> s b (h l)")
             if u // 2 == NUNIT // 2 - 1:
                 lo = 512 * hc + 256 * jp
                 store_eng.dma_start(out=o_dram[:, :, lo:lo + 256], in_=dst)
@@ -198,6 +194,8 @@ def tile_attention_pa_kernel(tc, hidden_states, cos, sin, w_qkv, out_0, out_1, o
         for u in range(NUNIT + LAG):
             if u < NUNIT:
                 transposes(u)
+            if u < LAG:
+                keep_clock(WARM_NEXT)
             if u >= LAG:
                 matmuls(u - LAG)
             if u < NUNIT:

@@ -27,8 +27,6 @@ GADD = True
 PLAIN_ENG = "v"
 LAG = 2
 STORE_Q = "sync"
-WARM_FIRST = 6
-WARM_NEXT = 3
 
 
 def tile_attention_pa_kernel(tc, hidden_states, cos, sin, w_qkv, out_0, out_1, out_2):
@@ -50,14 +48,6 @@ def tile_attention_pa_kernel(tc, hidden_states, cos, sin, w_qkv, out_0, out_1, o
         psum_a = ctx.enter_context(tc.psum_pool(name="psum_a", bufs=A_BANKS))
         ctx.enter_context(tc.manual_schedule())
         store_eng = {"sync": nc.sync, "gpsimd": nc.gpsimd, "scalar": nc.scalar}[STORE_Q]
-
-        warm_sb = const.tile([P, 512], BF16)
-        nc.vector.memset(warm_sb[:], 0.0)
-        warm_ps = psum_a.tile([P, 512], F32, tag="acc")
-
-        def keep_clock(n):
-            for i in range(n):
-                nc.tensor.matmul(out=warm_ps[:], lhsT=warm_sb[:, 0:P], rhs=warm_sb[:], start=True, stop=True)
 
         ident = const.tile([P, P], F32)
         make_identity(nc, ident[:])
@@ -87,7 +77,6 @@ def tile_attention_pa_kernel(tc, hidden_states, cos, sin, w_qkv, out_0, out_1, o
         xgf = xgrp[:].bitcast(F32)
         xc = const.tile([P, 1024], U32, align_bytes=64)
         xs = const.tile([P, 1024], U8, align_bytes=64)
-        keep_clock(WARM_FIRST)
         for g in range(4):
             tpx = psum_t.tile([P, 512], F32, tag="tp")
             for t in range(4):
@@ -99,19 +88,17 @@ def tile_attention_pa_kernel(tc, hidden_states, cos, sin, w_qkv, out_0, out_1, o
                 nc.scalar.copy(out=dst, in_=src)
             else:
                 nc.vector.tensor_copy(out=dst, in_=src)
-        keep_clock(WARM_NEXT)
         for hf in range(2):
             nc.vector.quantize_mx(out=xc[:, 512 * hf:512 * hf + 512].bitcast(FP8X4),
                                   scales=xs[:, 512 * hf:512 * hf + 512],
                                   in_=xgrp[:, 2048 * hf:2048 * hf + 2048])
 
-        cosd = const.tile([P, P], F32)
-        sind = const.tile([P, P], F32)
-        nc.vector.tensor_copy(out=cosd[:], in_=cos_raw[:])
+        table = const.tile([P, 2 * P], F32)
+        nc.vector.tensor_copy(out=table[:, 0:P], in_=cos_raw[:])
         sin_v = sin_raw[:].rearrange("p (i e) -> p i e", e=2)
-        sind_v = sind[:].rearrange("p (i e) -> p i e", e=2)
-        nc.vector.tensor_scalar_mul(out=sind_v[:, :, 0], in0=sin_v[:, :, 0], scalar1=-1.0)
-        nc.vector.tensor_copy(out=sind_v[:, :, 1], in_=sin_v[:, :, 1])
+        fac_v = table[:, P:2 * P].rearrange("p (i e) -> p i e", e=2)
+        nc.vector.tensor_copy(out=fac_v[:, :, 0], in_=sin_v[:, :, 1])
+        nc.vector.tensor_scalar_mul(out=fac_v[:, :, 1], in0=sin_v[:, :, 0], scalar1=-1.0)
 
         grps = {}
         codes = {}
@@ -164,19 +151,17 @@ def tile_attention_pa_kernel(tc, hidden_states, cos, sin, w_qkv, out_0, out_1, o
             ost = osts[u // 2]
             dst = ost[:].rearrange("p (b m) -> p b m", b=2)[:, :, 256 * jp:256 * jp + 256]
             if kind < 2:
-                t1 = rpool.tile([P, 512], F32, tag="t1")
-                t2 = rpool.tile([P, 512], F32, tag="t2")
-                nc.vector.tensor_tensor(out=t1[:].rearrange("p (h m) -> p h m", h=4),
-                                        in0=acc[:].rearrange("p (h m) -> p h m", h=4),
-                                        in1=cosd[:].unsqueeze(1).to_broadcast([P, 4, P]), op=MULT)
+                prod = rpool.tile([P, 1024], F32, tag="prod")
                 nc.vector.tensor_tensor(
-                    out=t2[:].rearrange("p (h i e) -> p h i e", h=4, e=2),
-                    in0=acc[:].rearrange("p (h i e) -> p h i e", h=4, e=2)[:, :, :, ::-1],
-                    in1=sind[:].rearrange("p (i e) -> p i e", e=2).unsqueeze(1).to_broadcast([P, 4, 64, 2]),
+                    out=prod[:].rearrange("p (w h m) -> p w h m", w=2, h=4),
+                    in0=acc[:].rearrange("p (h m) -> p h m", h=4).unsqueeze(1).to_broadcast([P, 2, 4, P]),
+                    in1=table[:].rearrange("p (w m) -> p w m", w=2).unsqueeze(2).to_broadcast([P, 2, 4, P]),
                     op=MULT)
-                add_eng = nc.gpsimd if GADD else nc.vector
-                add_eng.tensor_tensor(out=dst, in0=t1[:].rearrange("p (b m) -> p b m", b=2),
-                                      in1=t2[:].rearrange("p (b m) -> p b m", b=2), op=ADD)
+                nc.gpsimd.tensor_tensor(
+                    out=dst.rearrange("p b (r e) -> p b r e", e=2),
+                    in0=prod[:, 0:512].rearrange("p (b r e) -> p b r e", b=2, e=2),
+                    in1=prod[:, 512:1024].rearrange("p (b r e) -> p b r e", b=2, e=2)[:, :, :, ::-1],
+                    op=ADD)
             else:
                 src = acc[:].rearrange("p (b m) -> p b m", b=2)
                 if PLAIN_ENG == "s" or u >= NUNIT - 2:
@@ -194,8 +179,6 @@ def tile_attention_pa_kernel(tc, hidden_states, cos, sin, w_qkv, out_0, out_1, o
         for u in range(NUNIT + LAG):
             if u < NUNIT:
                 transposes(u)
-            if u < LAG:
-                keep_clock(WARM_NEXT)
             if u >= LAG:
                 matmuls(u - LAG)
             if u < NUNIT:

from contextlib import ExitStack

import concourse.mybir as mybir
from concourse.masks import make_identity

F32 = mybir.dt.float32
BF16 = mybir.dt.bfloat16
U32 = mybir.dt.uint32
U8 = mybir.dt.uint8
FP8X4 = mybir.dt.float8_e4m3fn_x4
MULT = mybir.AluOpType.mult
ADD = mybir.AluOpType.add

FLOPS = 2 * 256 * 6144 * 2048

P = 128
NUNIT = 24
W_BUFS = 12
GRP_BUFS = 4
CODE_BUFS = 4
OST_BUFS = 10
T_BANKS = 4
A_BANKS = 4
R_BUFS = 3
PATTERN = "RRRVRRRVRRVV"
GADD = True
PLAIN_ENG = "v"
LAG = 2
STORE_Q = "sync"


def tile_attention_pa_kernel(tc, hidden_states, cos, sin, w_qkv, out_0, out_1, out_2):
    nc = tc.nc
    outs = (out_0, out_1, out_2)
    rotated = [(kind, hc) for hc in range(4) for kind in range(2)]
    plain = [(2, hc) for hc in range(4)]
    groups = []
    for ch in PATTERN:
        groups.append(rotated.pop(0) if ch == "R" else plain.pop(0))
    with ExitStack() as ctx:
        const = ctx.enter_context(tc.tile_pool(name="const", bufs=1))
        wpool = ctx.enter_context(tc.tile_pool(name="wpool", bufs=W_BUFS))
        gpool = ctx.enter_context(tc.tile_pool(name="gpool", bufs=GRP_BUFS))
        cpool = ctx.enter_context(tc.tile_pool(name="cpool", bufs=CODE_BUFS))
        rpool = ctx.enter_context(tc.tile_pool(name="rpool", bufs=R_BUFS))
        opool = ctx.enter_context(tc.tile_pool(name="opool", bufs=OST_BUFS))
        psum_t = ctx.enter_context(tc.psum_pool(name="psum_t", bufs=T_BANKS))
        psum_a = ctx.enter_context(tc.psum_pool(name="psum_a", bufs=A_BANKS))
        ctx.enter_context(tc.manual_schedule())
        store_eng = {"sync": nc.sync, "gpsimd": nc.gpsimd, "scalar": nc.scalar}[STORE_Q]

        ident = const.tile([P, P], F32)
        make_identity(nc, ident[:])
        cos_raw = const.tile([P, P], BF16)
        sin_raw = const.tile([P, P], BF16)
        nc.scalar.dma_start(out=cos_raw[:], in_=cos)
        nc.scalar.dma_start(out=sin_raw[:], in_=sin)

        xraw = const.tile([P, 4096], BF16)
        x_dram = hidden_states.rearrange("b s k -> s b k")
        x_sb = xraw[:].rearrange("p (b k) -> p b k", b=2)
        for hf in range(2):
            nc.sync.dma_start(out=x_sb[:, :, 1024 * hf:1024 * hf + 1024],
                              in_=x_dram[:, :, 1024 * hf:1024 * hf + 1024])

        wraws = []
        for u in range(NUNIT):
            kind, hc = groups[u // 2]
            r0 = 2048 * kind + 512 * hc + 256 * (u % 2)
            wraw = wpool.tile([P, 4096], BF16)
            wraws.append(wraw)
            nc.sync.dma_start(out=wraw[:].rearrange("p (j k) -> p j k", j=2),
                              in_=w_qkv[r0:r0 + 256, :].rearrange("(j p) k -> p j k", j=2))

        xf = xraw[:].bitcast(F32)
        xgrp = const.tile([P, 4096], BF16, align_bytes=64)
        xgf = xgrp[:].bitcast(F32)
        xc = const.tile([P, 1024], U32, align_bytes=64)
        xs = const.tile([P, 1024], U8, align_bytes=64)
        for g in range(4):
            tpx = psum_t.tile([P, 512], F32, tag="tp")
            for t in range(4):
                o = 1024 * (t // 2) + 256 * g + 128 * (t % 2)
                nc.tensor.transpose(tpx[:, 128 * t:128 * t + 128], xf[:, o:o + 128], ident[:])
            dst = xgf[:, 512 * g:512 * g + 512].rearrange("q (b s u) -> q b s u", b=2, u=2)
            src = tpx[:].rearrange("q (b u s) -> q b s u", b=2, u=2)
            if g % 2 == 0:
                nc.scalar.copy(out=dst, in_=src)
            else:
                nc.vector.tensor_copy(out=dst, in_=src)
        for hf in range(2):
            nc.vector.quantize_mx(out=xc[:, 512 * hf:512 * hf + 512].bitcast(FP8X4),
                                  scales=xs[:, 512 * hf:512 * hf + 512],
                                  in_=xgrp[:, 2048 * hf:2048 * hf + 2048])

        table = const.tile([P, 2 * P], F32)
        nc.vector.tensor_copy(out=table[:, 0:P], in_=cos_raw[:])
        sin_v = sin_raw[:].rearrange("p (i e) -> p i e", e=2)
        fac_v = table[:, P:2 * P].rearrange("p (i e) -> p i e", e=2)
        nc.vector.tensor_copy(out=fac_v[:, :, 0], in_=sin_v[:, :, 1])
        nc.vector.tensor_scalar_mul(out=fac_v[:, :, 1], in0=sin_v[:, :, 0], scalar1=-1.0)

        grps = {}
        codes = {}
        accs = {}
        osts = {}

        def transposes(u):
            wf = wraws[u][:].bitcast(F32)
            grp = gpool.tile([P, 4096], BF16, align_bytes=64, tag="grp")
            grps[u] = grp
            gf = grp[:].bitcast(F32)
            for g in range(4):
                tp = psum_t.tile([P, 512], F32, tag="tp")
                for t in range(4):
                    o = 1024 * (t // 2) + 256 * g + 128 * (t % 2)
                    nc.tensor.transpose(tp[:, 128 * t:128 * t + 128], wf[:, o:o + 128], ident[:])
                nc.scalar.copy(out=gf[:, 512 * g:512 * g + 512].rearrange("q (j c u) -> q j c u", j=2, u=2),
                               in_=tp[:].rearrange("q (j u c) -> q j c u", j=2, u=2))

        def quantise(u):
            wc = cpool.tile([P, 1024], U32, align_bytes=64, tag="wc")
            ws = cpool.tile([P, 1024], U8, align_bytes=64, tag="ws")
            codes[u] = (wc, ws)
            pieces = 4 if u == NUNIT - 1 else 1
            n = 1024 // pieces
            for i in range(pieces):
                nc.vector.quantize_mx(out=wc[:, n * i:n * i + n].bitcast(FP8X4), scales=ws[:, n * i:n * i + n],
                                      in_=grps[u][:, 4 * n * i:4 * n * i + 4 * n])

        def matmuls(u):
            acc = psum_a.tile([P, 512], F32, tag="acc")
            accs[u] = acc
            wc, ws = codes[u]
            for b in range(2):
                for g in range(4):
                    xo = 256 * g + 128 * b
                    nc.tensor.matmul_mx(out=acc[:, 256 * b:256 * b + 256],
                                        lhsT=xc[:, xo:xo + 128].bitcast(FP8X4), lhsT_scale=xs[:, xo:xo + 128],
                                        rhs=wc[:, 256 * g:256 * g + 256].bitcast(FP8X4),
                                        rhs_scale=ws[:, 256 * g:256 * g + 256],
                                        start=(g == 0), stop=(g == 3))

        def finish(u):
            kind, hc = groups[u // 2]
            jp = u % 2
            acc = accs[u]
            if jp == 0:
                ost = opool.tile([P, 1024], F32, tag="ost")
                osts[u // 2] = ost
            ost = osts[u // 2]
            dst = ost[:].rearrange("p (b m) -> p b m", b=2)[:, :, 256 * jp:256 * jp + 256]
            if kind < 2:
                prod = rpool.tile([P, 1024], F32, tag="prod")
                nc.vector.tensor_tensor(
                    out=prod[:].rearrange("p (w h m) -> p w h m", w=2, h=4),
                    in0=acc[:].rearrange("p (h m) -> p h m", h=4).unsqueeze(1).to_broadcast([P, 2, 4, P]),
                    in1=table[:].rearrange("p (w m) -> p w m", w=2).unsqueeze(2).to_broadcast([P, 2, 4, P]),
                    op=MULT)
                nc.gpsimd.tensor_tensor(
                    out=dst.rearrange("p b (r e) -> p b r e", e=2),
                    in0=prod[:, 0:512].rearrange("p (b r e) -> p b r e", b=2, e=2),
                    in1=prod[:, 512:1024].rearrange("p (b r e) -> p b r e", b=2, e=2)[:, :, :, ::-1],
                    op=ADD)
            else:
                src = acc[:].rearrange("p (b m) -> p b m", b=2)
                if PLAIN_ENG == "s" or u >= NUNIT - 2:
                    nc.scalar.copy(out=dst, in_=src)
                else:
                    nc.vector.tensor_copy(out=dst, in_=src)
            o_dram = outs[kind].rearrange("b s h l -> s b (h l)")
            if u // 2 == NUNIT // 2 - 1:
                lo = 512 * hc + 256 * jp
                store_eng.dma_start(out=o_dram[:, :, lo:lo + 256], in_=dst)
            elif jp == 1:
                store_eng.dma_start(out=o_dram[:, :, 512 * hc:512 * hc + 512],
                                    in_=ost[:].rearrange("p (b m) -> p b m", b=2))

        for u in range(NUNIT + LAG):
            if u < NUNIT:
                transposes(u)
            if u >= LAG:
                matmuls(u - LAG)
            if u < NUNIT:
                quantise(u)
            if u >= LAG:
                finish(u - LAG)
